import numpy as np
import ml_dtypes


def mxq(x, axis, fmt="e4m3"):
    dtype, down = {"e4m3": (ml_dtypes.float8_e4m3fn, 7), "e5m2": (ml_dtypes.float8_e5m2, 14)}[fmt]
    v = np.moveaxis(np.asarray(x, np.float32).astype(ml_dtypes.bfloat16).astype(np.float64), axis, -1)
    blocks = v.reshape(v.shape[:-1] + (-1, 32))
    amax = np.abs(blocks).max(-1, keepdims=True)
    byte = np.maximum(np.where(amax > 0, np.frexp(amax)[1] - 1 + 127, 0) - down, 1)
    scale = np.exp2(byte - 127.0)
    codes = (blocks / scale).astype(np.float32).astype(dtype).astype(np.float64)
    return np.moveaxis((codes * scale).reshape(v.shape), -1, axis)


WIDE = False


def mx_kscale(k):
    if not WIDE:
        return np.ones(k)
    levels = np.array([10, -10, 5, -5, 0])
    if k % 512:
        return np.exp2(np.random.permutation(np.resize(levels, k // 32))).repeat(32)
    a = np.empty((k // 512, 16))
    for p in range(k // 512):
        a[p, :8] = np.random.permutation(np.resize(levels, 8))
        for g in range(8):
            far = levels[np.abs(levels - a[p, g]) >= 10]
            a[p, g + 8] = far[np.random.randint(len(far))]
    return np.exp2(a.ravel()).repeat(32)


BF16 = ml_dtypes.bfloat16


def bf(x):
    return np.asarray(x, np.float32).astype(BF16)


def f64(x):
    return np.asarray(x).astype(np.float64)


B, K, C, H, W = 4, 64, 256, 96, 128
P = H * W
EPS = 1e-12


def setup_inputs():
    s = mx_kscale(P).reshape(H, W)
    cw = 0.2 + 0.8 * np.random.random_sample((B, K))
    return {"preds": bf(np.random.random_sample((B, K, H, W)) * cw[:, :, None, None] * s),
            "feats": bf(np.random.standard_normal((B, C, H, W)) / s)}


def reference(preds, feats):
    p = f64(preds).reshape(B, K, P)
    f = f64(feats).reshape(B, C, P)
    vec = (mxq(p, 2, "e4m3") @ mxq(f, 2, "e4m3").transpose(0, 2, 1)) / p.sum(-1)[..., None]
    norm = np.maximum(np.sqrt((vec ** 2).sum(1, keepdims=True)), EPS)
    return vec / norm

@@ -1,0 +1,288 @@
+from contextlib import ExitStack
+
+import concourse.mybir as mybir
+from concourse.masks import make_identity
+
+F32 = mybir.dt.float32
+BF16 = mybir.dt.bfloat16
+U32 = mybir.dt.uint32
+U8 = mybir.dt.uint8
+FP8X4 = mybir.dt.float8_e4m3fn_x4
+ALU = mybir.AluOpType
+ACT = mybir.ActivationFunctionType
+AX = mybir.AxisListType
+
+FLOPS = 2 * 4 * 64 * 256 * 12288
+
+P = 128
+PASS = 512
+STEP = 2 * PASS
+PIXELS = 12288
+PAIR_STEPS = PIXELS // STEP
+N_STEPS = 2 * PAIR_STEPS
+LEAD = 2
+AHEAD = 10
+FEATS_BLOCKS = [1, 1] + [2] * 10 + [1, 1]
+PREDS_BLOCK = 4
+EPS = 1e-12
+
+
+def tile_categoryalign_module_pa_kernel(tc, preds, feats, out):
+    nc = tc.nc
+    pf = preds.rearrange("b k h w -> (b k) (h w)")
+    ff = feats.rearrange("b c h w -> (b c) (h w)")
+    of = out.rearrange("b k c -> (b k) c")
+
+    with ExitStack() as ctx:
+        const = ctx.enter_context(tc.tile_pool(name="const", bufs=1))
+        raw_pool = ctx.enter_context(tc.tile_pool(name="raw_pool", bufs=1))
+        work = ctx.enter_context(tc.tile_pool(name="work", bufs=1))
+        tail = ctx.enter_context(tc.tile_pool(name="tail", bufs=2))
+        psum = ctx.enter_context(tc.psum_pool(name="psum", bufs=1))
+        ctx.enter_context(tc.manual_schedule())
+
+        loads = []
+        for m in range(N_STEPS // PREDS_BLOCK):
+            loads.append((PREDS_BLOCK * m - LEAD, 0, m))
+        first = 0
+        for width in FEATS_BLOCKS:
+            loads.append((first, 1, width))
+            first += width
+        loads = sorted(loads)
+        preds_raw = {}
+        feats_raw = {}
+
+        def start_load(first_step, is_feats, arg):
+            if is_feats:
+                pair, local = divmod(first_step, PAIR_STEPS)
+                cols = STEP * arg
+                r = raw_pool.tile([P, 4 * STEP * max(FEATS_BLOCKS)], BF16, tag="rf", bufs=6, name="rf")
+                src = ff[4 * P * pair : 4 * P * (pair + 1), STEP * local : STEP * local + cols].rearrange(
+                    "(j p) x -> p j x", p=P
+                )
+                dst = r[:, 0 : 4 * cols].rearrange("p (j x) -> p j x", j=4)
+                if first_step == 0 or first_step + arg == N_STEPS:
+                    for j in range(4):
+                        nc.sync.dma_start(out=dst[:, j], in_=src[:, j])
+                else:
+                    nc.sync.dma_start(out=dst, in_=src)
+                for i in range(arg):
+                    feats_raw[first_step + i] = (r[:].bitcast(F32), (STEP // 2) * i, cols // 2)
+            else:
+                sigma = PREDS_BLOCK * arg
+                pair, local = divmod(sigma, PAIR_STEPS)
+                cols = STEP * PREDS_BLOCK
+                r = raw_pool.tile([P, cols], BF16, tag="rp", bufs=4, name="rp")
+                pieces = PREDS_BLOCK if arg == 0 else 1
+                for i in range(pieces):
+                    lo = cols // pieces * i
+                    hi = cols // pieces * (i + 1)
+                    nc.sync.dma_start(
+                        out=r[:, lo:hi], in_=pf[P * pair : P * (pair + 1), STEP * local + lo : STEP * local + hi]
+                    )
+                for i in range(PREDS_BLOCK):
+                    preds_raw[sigma + i] = (r[:].bitcast(F32), (STEP // 2) * i)
+
+        n_started = 0
+        while n_started < len(loads) and loads[n_started][0] <= AHEAD - LEAD:
+            start_load(*loads[n_started])
+            n_started += 1
+
+        ident = const.tile([P, P], F32, name="ident")
+        make_identity(nc, ident[:])
+        ones = const.tile([P, 2], BF16, name="ones")
+        nc.vector.memset(ones[:], 1.0)
+        fold = const.tile([P, 32], F32, name="fold")
+        nc.vector.tensor_reduce(out=fold[:], in_=ident[:].rearrange("p (a t) -> p a t", t=4), axis=AX.X, op=ALU.add)
+        sel = const.tile([P, 4 * P], F32, name="sel")
+        nc.vector.memset(sel[:], 0.0)
+        for j in range(4):
+            nc.vector.tensor_copy(out=sel[:, (P + 32) * j : (P + 32) * j + 32], in_=fold[:])
+        same_image = const.tile([P, P], F32, name="same_image")
+        nc.vector.memset(same_image[:], 0.0)
+        nc.vector.memset(same_image[0:64, 0:64], 1.0)
+        nc.vector.memset(same_image[64:128, 64:128], 1.0)
+        one_col = const.tile([P, 1], F32, name="one_col")
+        nc.vector.memset(one_col[:], 1.0)
+        table_warm = const.tile([P, 1], F32, name="table_warm")
+        nc.scalar.activation(out=table_warm[:], in_=one_col[:], func=ACT.Abs_reciprocal_sqrt)
+
+        sums = psum.tile([P, 512], F32, tag="sums", name="sums")
+        preds_grouped = {}
+        feats_grouped = {}
+        preds_codes = {}
+        feats_codes = {}
+        acc = {}
+        keep = {}
+
+        def live(x):
+            return 0 <= x < N_STEPS
+
+        def transpose_bank(words, word0, dst, copy):
+            bank = psum.tile([P, 512], F32, tag="bank", bufs=6, name="bank")
+            for a in range(2):
+                for u in range(2):
+                    k = 2 * a + u
+                    w = word0 + 256 * a
+                    nc.tensor.transpose(bank[:, P * k : P * k + P], words[:, w + u : w + 256 : 2], ident[:])
+            copy(out=dst, in_=bank[:].rearrange("p (a u r) -> p a r u", a=2, u=2))
+
+        def transpose_preds(sigma):
+            g = work.tile([P, 4 * 2 * P], BF16, tag="pg", bufs=3, name="pg", align_bytes=64)
+            preds_grouped[sigma] = g
+            words, word0 = preds_raw[sigma]
+            transpose_bank(words, word0, g[:].bitcast(F32).rearrange("p (a r u) -> p a r u", a=2, u=2), nc.scalar.copy)
+
+        def transpose_feats(s, row_tiles):
+            if s not in feats_grouped:
+                feats_grouped[s] = work.tile([P, 4 * 2 * 4 * P], BF16, tag="fg", bufs=3, name="fg", align_bytes=64)
+            words, word0, pitch = feats_raw[s]
+            view = feats_grouped[s][:].bitcast(F32).rearrange("p (a j r u) -> p a j r u", a=2, j=4, u=2)
+            for j in row_tiles:
+                transpose_bank(
+                    words, word0 + pitch * j, view[:, :, j], nc.vector.tensor_copy if j == 3 else nc.scalar.copy
+                )
+
+        def quantise(grouped, tag, bufs):
+            width = grouped.shape[1] // 4
+            codes = work.tile([P, width], U32, tag=tag + "c", bufs=bufs, name=tag + "c", align_bytes=64)
+            scales = work.tile([P, width], U8, tag=tag + "s", bufs=bufs, name=tag + "s", align_bytes=64)
+            nc.vector.quantize_mx(out=codes[:].bitcast(FP8X4), scales=scales[:], in_=grouped[:])
+            return codes, scales
+
+        def pixel_sums(sigma, quarter):
+            pair, local = divmod(sigma, PAIR_STEPS)
+            a, half = divmod(quarter, 2)
+            for j in (2 * half, 2 * half + 1):
+                col = 96 * pair + 24 * j + 2 * local + a
+                nc.tensor.matmul(
+                    out=sums[:, col : col + 1],
+                    lhsT=preds_grouped[sigma][:, 512 * a + P * j : 512 * a + P * j + P],
+                    rhs=ones[:, 0:1],
+                    start=True,
+                    stop=True,
+                )
+
+        def mx_pass(s, a):
+            pair, local = divmod(s, PAIR_STEPS)
+            if local == 0 and a == 0:
+                acc[pair] = psum.tile([P, 512], F32, tag="acc", name="acc")
+            pc, ps = preds_codes[s]
+            fc, fs = feats_codes[s]
+            nc.tensor.matmul_mx(
+                out=acc[pair][:],
+                lhsT=pc[:, P * a : P * a + P].bitcast(FP8X4),
+                lhsT_scale=ps[:, P * a : P * a + P],
+                rhs=fc[:, 512 * a : 512 * a + 512].bitcast(FP8X4),
+                rhs_scale=fs[:, 512 * a : 512 * a + 512],
+                start=(local == 0 and a == 0),
+                stop=(local == PAIR_STEPS - 1 and a == 1),
+            )
+
+        def denominator_fold(pair):
+            part = tail.tile([P, 4], F32, tag="part", name="part")
+            nc.vector.tensor_reduce(
+                out=part[:],
+                in_=sums[:, 96 * pair : 96 * pair + 96].rearrange("p (j x) -> p j x", j=4),
+                axis=AX.X,
+                op=ALU.add,
+            )
+            keep[("part", pair)] = part
+
+        def denominator_place(pair):
+            for j in range(4):
+                nc.tensor.matmul(
+                    out=sums[:, 192 + pair : 193 + pair],
+                    lhsT=sel[:, P * j : P * j + P],
+                    rhs=keep[("part", pair)][:, j : j + 1],
+                    start=(j == 0),
+                    stop=(j == 3),
+                )
+
+        def denominator_invert(pair):
+            rd = tail.tile([P, 1], F32, tag="rd", name="rd")
+            nc.vector.reciprocal(out=rd[:], in_=sums[:, 192 + pair : 193 + pair])
+            keep[("rd", pair)] = rd
+
+        def finish_square(pair):
+            rd = keep[("rd", pair)]
+            sq = tail.tile([P, 256], F32, tag="sq", name="sq")
+            vec = tail.tile([P, 256], F32, tag="vec", name="vec")
+            for h in range(2):
+                rows = slice(64 * h, 64 * h + 64)
+                cols = slice(256 * h, 256 * h + 256)
+                nc.scalar.activation(out=sq[rows, :], in_=acc[pair][rows, cols], func=ACT.Square, scale=rd[rows, 0:1])
+            for h in range(2):
+                rows = slice(64 * h, 64 * h + 64)
+                cols = slice(256 * h, 256 * h + 256)
+                nc.vector.tensor_scalar_mul(out=vec[rows, :], in0=acc[pair][rows, cols], scalar1=rd[rows, 0:1])
+            keep[("sq", pair)] = sq
+            keep[("vec", pair)] = vec
+
+        def finish_norm(pair):
+            bank = psum.tile([P, 512], F32, tag="bank", bufs=6, name="bank")
+            nc.tensor.matmul(out=bank[:, 0:256], lhsT=same_image[:], rhs=keep[("sq", pair)][:], start=True, stop=True)
+            keep[("nsq", pair)] = bank
+
+        def finish_root(pair):
+            rn = tail.tile([P, 256], F32, tag="rn", name="rn")
+            nc.scalar.activation(out=rn[:], in_=keep[("nsq", pair)][:, 0:256], func=ACT.Abs_reciprocal_sqrt)
+            keep[("rn", pair)] = rn
+
+        def finish_store(pair):
+            res = tail.tile([P, 256], F32, tag="res", name="res")
+            nc.vector.scalar_tensor_tensor(
+                out=res[:],
+                in0=keep[("rn", pair)][:],
+                scalar=1.0 / EPS,
+                in1=keep[("vec", pair)][:],
+                op0=ALU.min,
+                op1=ALU.mult,
+            )
+            nc.sync.dma_start(out=of[P * pair : P * pair + P, :], in_=res[:])
+
+        for s in range(-LEAD, N_STEPS + 6):
+            sigma = s + LEAD
+            for pair in range(2):
+                summed = PAIR_STEPS * (pair + 1) - LEAD
+                closed = PAIR_STEPS * (pair + 1) + 1
+                if s == summed + 1:
+                    denominator_fold(pair)
+                if s == summed + 2:
+                    denominator_invert(pair)
+                if s == closed + 1:
+                    finish_square(pair)
+                if s == closed + 2:
+                    finish_root(pair)
+                if s == closed + 3:
+                    finish_store(pair)
+            if live(sigma - 1):
+                preds_codes[sigma - 1] = quantise(preds_grouped[sigma - 1], "p", 8)
+            if live(s - 1):
+                feats_codes[s - 1] = quantise(feats_grouped[s - 1], "f", 4)
+            if live(sigma):
+                transpose_preds(sigma)
+            if live(s):
+                transpose_feats(s, (0, 1))
+            if live(sigma - 1):
+                pixel_sums(sigma - 1, 0)
+            if live(s - 2):
+                mx_pass(s - 2, 0)
+            if live(sigma - 1):
+                pixel_sums(sigma - 1, 1)
+            if live(s):
+                transpose_feats(s, (2, 3))
+            while n_started < len(loads) and loads[n_started][0] <= s + AHEAD:
+                start_load(*loads[n_started])
+                n_started += 1
+            if live(sigma - 1):
+                pixel_sums(sigma - 1, 2)
+            for pair in range(2):
+                if s == PAIR_STEPS * (pair + 1) - LEAD + 1:
+                    denominator_place(pair)
+                if s == PAIR_STEPS * (pair + 1) + 2:
+                    finish_norm(pair)
+            if live(s - 2):
+                mx_pass(s - 2, 1)
+            if live(sigma - 1):
+                pixel_sums(sigma - 1, 3)

@@ -20,10 +20,10 @@ STEP = 2 * PASS
 PIXELS = 12288
 PAIR_STEPS = PIXELS // STEP
 N_STEPS = 2 * PAIR_STEPS
-LEAD = 2
+LEAD = 1
 AHEAD = 10
-FEATS_BLOCKS = [1, 1] + [2] * 10 + [1, 1]
-PREDS_BLOCK = 4
+FEATS_BLOCKS = [1, 1, 1, 1] + [2] * 9 + [1, 1]
+PREDS_BLOCKS = [1, 1, 2] + [4] * 5
 EPS = 1e-12
 
 
@@ -42,8 +42,10 @@ def tile_categoryalign_module_pa_kernel(tc, preds, feats, out):
         ctx.enter_context(tc.manual_schedule())
 
         loads = []
-        for m in range(N_STEPS // PREDS_BLOCK):
-            loads.append((PREDS_BLOCK * m - LEAD, 0, m))
+        first = 0
+        for width in PREDS_BLOCKS:
+            loads.append((first - LEAD, 0, width))
+            first += width
         first = 0
         for width in FEATS_BLOCKS:
             loads.append((first, 1, width))
@@ -69,18 +71,14 @@ def tile_categoryalign_module_pa_kernel(tc, preds, feats, out):
                 for i in range(arg):
                     feats_raw[first_step + i] = (r[:].bitcast(F32), (STEP // 2) * i, cols // 2)
             else:
-                sigma = PREDS_BLOCK * arg
+                sigma = first_step + LEAD
                 pair, local = divmod(sigma, PAIR_STEPS)
-                cols = STEP * PREDS_BLOCK
-                r = raw_pool.tile([P, cols], BF16, tag="rp", bufs=4, name="rp")
-                pieces = PREDS_BLOCK if arg == 0 else 1
-                for i in range(pieces):
-                    lo = cols // pieces * i
-                    hi = cols // pieces * (i + 1)
-                    nc.sync.dma_start(
-                        out=r[:, lo:hi], in_=pf[P * pair : P * (pair + 1), STEP * local + lo : STEP * local + hi]
-                    )
-                for i in range(PREDS_BLOCK):
+                cols = STEP * arg
+                r = raw_pool.tile([P, STEP * max(PREDS_BLOCKS)], BF16, tag="rp", bufs=4, name="rp")
+                nc.sync.dma_start(
+                    out=r[:, 0:cols], in_=pf[P * pair : P * (pair + 1), STEP * local : STEP * local + cols]
+                )
+                for i in range(arg):
                     preds_raw[sigma + i] = (r[:].bitcast(F32), (STEP // 2) * i)
 
         n_started = 0
@@ -108,6 +106,8 @@ def tile_categoryalign_module_pa_kernel(tc, preds, feats, out):
         nc.scalar.activation(out=table_warm[:], in_=one_col[:], func=ACT.Abs_reciprocal_sqrt)
 
         sums = psum.tile([P, 512], F32, tag="sums", name="sums")
+        preds_shuffled = {}
+        feats_shuffled = {}
         preds_grouped = {}
         feats_grouped = {}
         preds_codes = {}
@@ -118,30 +118,65 @@ def tile_categoryalign_module_pa_kernel(tc, preds, feats, out):
         def live(x):
             return 0 <= x < N_STEPS
 
-        def transpose_bank(words, word0, dst, copy):
+        def shuffled(step):
+            return 2 <= step < N_STEPS - 1
+
+        def shuffle_preds(step):
+            words, word0 = preds_raw[step]
+            t = work.tile([P, STEP], BF16, tag="sp", bufs=3, name="sp")
+            raw = words.bitcast(BF16)[:, 2 * word0 : 2 * word0 + STEP]
+            nc.vector.tensor_copy(
+                out=t[:].rearrange("p (u x e) -> p u x e", u=2, e=16),
+                in_=raw.rearrange("p (x u e) -> p u x e", u=2, e=16),
+            )
+            preds_shuffled[step] = t[:].bitcast(F32)
+
+        def shuffle_feats(step):
+            words, word0, pitch = feats_raw[step]
+            t = work.tile([P, 4 * STEP], BF16, tag="sf", bufs=3, name="sf")
+            raw = words.bitcast(BF16)[:, 0 : 8 * pitch].rearrange("p (j c) -> p j c", j=4)
+            raw = raw[:, :, 2 * word0 : 2 * word0 + STEP].rearrange("p j (x u e) -> p u j x e", u=2, e=16)
+            dst = t[:].rearrange("p (u j x e) -> p u j x e", u=2, j=4, e=16)
+            for u in range(2):
+                nc.vector.tensor_copy(out=dst[:, u], in_=raw[:, u])
+            feats_shuffled[step] = t[:].bitcast(F32)
+
+        def transpose_bank(windows, dst, copy):
             bank = psum.tile([P, 512], F32, tag="bank", bufs=6, name="bank")
             for a in range(2):
                 for u in range(2):
                     k = 2 * a + u
-                    w = word0 + 256 * a
-                    nc.tensor.transpose(bank[:, P * k : P * k + P], words[:, w + u : w + 256 : 2], ident[:])
+                    nc.tensor.transpose(bank[:, P * k : P * k + P], windows[a][u], ident[:])
             copy(out=dst, in_=bank[:].rearrange("p (a u r) -> p a r u", a=2, u=2))
+
+        def every_second(words, word0):
+            return [[words[:, word0 + 256 * a + u : word0 + 256 * a + 256 : 2] for u in range(2)] for a in range(2)]
+
+        def contiguous(words, word0, apart):
+            return [[words[:, word0 + apart * u + P * a : word0 + apart * u + P * a + P] for u in range(2)] for a in range(2)]
 
         def transpose_preds(sigma):
             g = work.tile([P, 4 * 2 * P], BF16, tag="pg", bufs=3, name="pg", align_bytes=64)
             preds_grouped[sigma] = g
-            words, word0 = preds_raw[sigma]
-            transpose_bank(words, word0, g[:].bitcast(F32).rearrange("p (a r u) -> p a r u", a=2, u=2), nc.scalar.copy)
+            if shuffled(sigma):
+                windows = contiguous(preds_shuffled[sigma], 0, STEP // 4)
+            else:
+                windows = every_second(*preds_raw[sigma])
+            transpose_bank(windows, g[:].bitcast(F32).rearrange("p (a r u) -> p a r u", a=2, u=2), nc.scalar.copy)
 
         def transpose_feats(s, row_tiles):
             if s not in feats_grouped:
                 feats_grouped[s] = work.tile([P, 4 * 2 * 4 * P], BF16, tag="fg", bufs=3, name="fg", align_bytes=64)
-            words, word0, pitch = feats_raw[s]
             view = feats_grouped[s][:].bitcast(F32).rearrange("p (a j r u) -> p a j r u", a=2, j=4, u=2)
             for j in row_tiles:
-                transpose_bank(
-                    words, word0 + pitch * j, view[:, :, j], nc.vector.tensor_copy if j == 3 else nc.scalar.copy
-                )
+                if shuffled(s):
+                    windows = contiguous(feats_shuffled[s], STEP // 4 * j, STEP)
+                    copy = nc.scalar.copy
+                else:
+                    words, word0, pitch = feats_raw[s]
+                    windows = every_second(words, word0 + pitch * j)
+                    copy = nc.vector.tensor_copy if j % 2 == 1 else nc.scalar.copy
+                transpose_bank(windows, view[:, :, j], copy)
 
         def quantise(grouped, tag, bufs):
             width = grouped.shape[1] // 4
@@ -256,6 +291,10 @@ def tile_categoryalign_module_pa_kernel(tc, preds, feats, out):
                     finish_root(pair)
                 if s == closed + 3:
                     finish_store(pair)
+            if live(s + 1) and shuffled(s + 1):
+                shuffle_feats(s + 1)
+            if live(sigma + 1) and shuffled(sigma + 1):
+                shuffle_preds(sigma + 1)
             if live(sigma - 1):
                 preds_codes[sigma - 1] = quantise(preds_grouped[sigma - 1], "p", 8)
             if live(s - 1):

@@ -123,8 +123,8 @@ def tile_categoryalign_module_pa_kernel(tc, preds, feats, out):
 
         def shuffle_preds(step):
             words, word0 = preds_raw[step]
-            t = work.tile([P, STEP], BF16, tag="sp", bufs=3, name="sp")
-            raw = words.bitcast(BF16)[:, 2 * word0 : 2 * word0 + STEP]
+            t = work.tile([P, PASS], BF16, tag="sp", bufs=3, name="sp")
+            raw = words.bitcast(BF16)[:, 2 * word0 + PASS : 2 * word0 + STEP]
             nc.vector.tensor_copy(
                 out=t[:].rearrange("p (u x e) -> p u x e", u=2, e=16),
                 in_=raw.rearrange("p (x u e) -> p u x e", u=2, e=16),
@@ -133,9 +133,9 @@ def tile_categoryalign_module_pa_kernel(tc, preds, feats, out):
 
         def shuffle_feats(step):
             words, word0, pitch = feats_raw[step]
-            t = work.tile([P, 4 * STEP], BF16, tag="sf", bufs=3, name="sf")
+            t = work.tile([P, 4 * PASS], BF16, tag="sf", bufs=3, name="sf")
             raw = words.bitcast(BF16)[:, 0 : 8 * pitch].rearrange("p (j c) -> p j c", j=4)
-            raw = raw[:, :, 2 * word0 : 2 * word0 + STEP].rearrange("p j (x u e) -> p u j x e", u=2, e=16)
+            raw = raw[:, :, 2 * word0 + PASS : 2 * word0 + STEP].rearrange("p j (x u e) -> p u j x e", u=2, e=16)
             dst = t[:].rearrange("p (u j x e) -> p u j x e", u=2, j=4, e=16)
             for u in range(2):
                 nc.vector.tensor_copy(out=dst[:, u], in_=raw[:, u])
@@ -150,18 +150,20 @@ def tile_categoryalign_module_pa_kernel(tc, preds, feats, out):
             copy(out=dst, in_=bank[:].rearrange("p (a u r) -> p a r u", a=2, u=2))
 
         def every_second(words, word0):
-            return [[words[:, word0 + 256 * a + u : word0 + 256 * a + 256 : 2] for u in range(2)] for a in range(2)]
+            return [words[:, word0 + u : word0 + 256 : 2] for u in range(2)]
 
         def contiguous(words, word0, apart):
-            return [[words[:, word0 + apart * u + P * a : word0 + apart * u + P * a + P] for u in range(2)] for a in range(2)]
+            return [words[:, word0 + apart * u : word0 + apart * u + P] for u in range(2)]
 
         def transpose_preds(sigma):
             g = work.tile([P, 4 * 2 * P], BF16, tag="pg", bufs=3, name="pg", align_bytes=64)
             preds_grouped[sigma] = g
+            words, word0 = preds_raw[sigma]
+            windows = [every_second(words, word0)]
             if shuffled(sigma):
-                windows = contiguous(preds_shuffled[sigma], 0, STEP // 4)
+                windows.append(contiguous(preds_shuffled[sigma], 0, PASS // 4))
             else:
-                windows = every_second(*preds_raw[sigma])
+                windows.append(every_second(words, word0 + 256))
             transpose_bank(windows, g[:].bitcast(F32).rearrange("p (a r u) -> p a r u", a=2, u=2), nc.scalar.copy)
 
         def transpose_feats(s, row_tiles):
@@ -169,14 +171,13 @@ def tile_categoryalign_module_pa_kernel(tc, preds, feats, out):
                 feats_grouped[s] = work.tile([P, 4 * 2 * 4 * P], BF16, tag="fg", bufs=3, name="fg", align_bytes=64)
             view = feats_grouped[s][:].bitcast(F32).rearrange("p (a j r u) -> p a j r u", a=2, j=4, u=2)
             for j in row_tiles:
+                words, word0, pitch = feats_raw[s]
+                windows = [every_second(words, word0 + pitch * j)]
                 if shuffled(s):
-                    windows = contiguous(feats_shuffled[s], STEP // 4 * j, STEP)
-                    copy = nc.scalar.copy
+                    windows.append(contiguous(feats_shuffled[s], PASS // 4 * j, PASS))
                 else:
-                    words, word0, pitch = feats_raw[s]
-                    windows = every_second(words, word0 + pitch * j)
-                    copy = nc.vector.tensor_copy if j % 2 == 1 else nc.scalar.copy
-                transpose_bank(windows, view[:, :, j], copy)
+                    windows.append(every_second(words, word0 + pitch * j + 256))
+                transpose_bank(windows, view[:, :, j], nc.vector.tensor_copy if j == 3 else nc.scalar.copy)
 
         def quantise(grouped, tag, bufs):
             width = grouped.shape[1] // 4

@@ -22,8 +22,8 @@ PAIR_STEPS = PIXELS // STEP
 N_STEPS = 2 * PAIR_STEPS
 LEAD = 1
 AHEAD = 10
-FEATS_BLOCKS = [1, 1, 1, 1] + [2] * 9 + [1, 1]
-PREDS_BLOCKS = [1, 1, 2] + [4] * 5
+FEATS_BLOCKS = [1] * 24
+PREDS_BLOCKS = [1] * 6 + [2] * 9
 EPS = 1e-12
 
 
@@ -58,7 +58,7 @@ def tile_categoryalign_module_pa_kernel(tc, preds, feats, out):
             if is_feats:
                 pair, local = divmod(first_step, PAIR_STEPS)
                 cols = STEP * arg
-                r = raw_pool.tile([P, 4 * STEP * max(FEATS_BLOCKS)], BF16, tag="rf", bufs=6, name="rf")
+                r = raw_pool.tile([P, 4 * STEP * max(FEATS_BLOCKS)], BF16, tag="rf", bufs=12, name="rf")
                 src = ff[4 * P * pair : 4 * P * (pair + 1), STEP * local : STEP * local + cols].rearrange(
                     "(j p) x -> p j x", p=P
                 )
@@ -74,7 +74,7 @@ def tile_categoryalign_module_pa_kernel(tc, preds, feats, out):
                 sigma = first_step + LEAD
                 pair, local = divmod(sigma, PAIR_STEPS)
                 cols = STEP * arg
-                r = raw_pool.tile([P, STEP * max(PREDS_BLOCKS)], BF16, tag="rp", bufs=4, name="rp")
+                r = raw_pool.tile([P, STEP * max(PREDS_BLOCKS)], BF16, tag="rp", bufs=8, name="rp")
                 nc.sync.dma_start(
                     out=r[:, 0:cols], in_=pf[P * pair : P * (pair + 1), STEP * local : STEP * local + cols]
                 )
@@ -244,16 +244,26 @@ def tile_categoryalign_module_pa_kernel(tc, preds, feats, out):
             rd = keep[("rd", pair)]
             sq = tail.tile([P, 256], F32, tag="sq", name="sq")
             vec = tail.tile([P, 256], F32, tag="vec", name="vec")
-            for h in range(2):
-                rows = slice(64 * h, 64 * h + 64)
-                cols = slice(256 * h, 256 * h + 256)
-                nc.scalar.activation(out=sq[rows, :], in_=acc[pair][rows, cols], func=ACT.Square, scale=rd[rows, 0:1])
-            for h in range(2):
-                rows = slice(64 * h, 64 * h + 64)
-                cols = slice(256 * h, 256 * h + 256)
-                nc.vector.tensor_scalar_mul(out=vec[rows, :], in0=acc[pair][rows, cols], scalar1=rd[rows, 0:1])
             keep[("sq", pair)] = sq
             keep[("vec", pair)] = vec
+            for h in range(2):
+                rows = slice(64 * h, 64 * h + 64)
+                cols = slice(256 * h, 256 * h + 256)
+                if pair == 0:
+                    nc.scalar.activation(out=vec[rows, :], in_=acc[pair][rows, cols], func=ACT.Copy, scale=rd[rows, 0:1])
+                else:
+                    nc.scalar.activation(
+                        out=sq[rows, :], in_=acc[pair][rows, cols], func=ACT.Square, scale=rd[rows, 0:1]
+                    )
+            if pair == 1:
+                for h in range(2):
+                    rows = slice(64 * h, 64 * h + 64)
+                    cols = slice(256 * h, 256 * h + 256)
+                    nc.vector.tensor_scalar_mul(out=vec[rows, :], in0=acc[pair][rows, cols], scalar1=rd[rows, 0:1])
+
+        def finish_square_of_vec(pair):
+            vec = keep[("vec", pair)]
+            nc.vector.tensor_tensor(out=keep[("sq", pair)][:], in0=vec[:], in1=vec[:], op=ALU.mult)
 
         def finish_norm(pair):
             bank = psum.tile([P, 512], F32, tag="bank", bufs=6, name="bank")
@@ -288,9 +298,12 @@ def tile_categoryalign_module_pa_kernel(tc, preds, feats, out):
                     denominator_invert(pair)
                 if s == closed + 1:
                     finish_square(pair)
-                if s == closed + 2:
+                late = 1 - pair
+                if pair == 0 and s == closed + 2:
+                    finish_square_of_vec(pair)
+                if s == closed + 2 + late:
                     finish_root(pair)
-                if s == closed + 3:
+                if s == closed + 3 + late:
                     finish_store(pair)
             if live(s + 1) and shuffled(s + 1):
                 shuffle_feats(s + 1)
@@ -303,26 +316,22 @@ def tile_categoryalign_module_pa_kernel(tc, preds, feats, out):
             if live(sigma):
                 transpose_preds(sigma)
             if live(s):
-                transpose_feats(s, (0, 1))
-            if live(sigma - 1):
-                pixel_sums(sigma - 1, 0)
-            if live(s - 2):
-                mx_pass(s - 2, 0)
-            if live(sigma - 1):
-                pixel_sums(sigma - 1, 1)
-            if live(s):
-                transpose_feats(s, (2, 3))
+                transpose_feats(s, (0, 1, 2, 3))
             while n_started < len(loads) and loads[n_started][0] <= s + AHEAD:
                 start_load(*loads[n_started])
                 n_started += 1
+            opens = s - 2 == PAIR_STEPS
+            if live(s - 2) and not opens:
+                mx_pass(s - 2, 0)
             if live(sigma - 1):
-                pixel_sums(sigma - 1, 2)
+                for quarter in range(4):
+                    pixel_sums(sigma - 1, quarter)
+            if live(s - 2):
+                if opens:
+                    mx_pass(s - 2, 0)
+                mx_pass(s - 2, 1)
             for pair in range(2):
                 if s == PAIR_STEPS * (pair + 1) - LEAD + 1:
                     denominator_place(pair)
-                if s == PAIR_STEPS * (pair + 1) + 2:
+                if s == PAIR_STEPS * (pair + 1) + 3 - pair:
                     finish_norm(pair)
-            if live(s - 2):
-                mx_pass(s - 2, 1)
-            if live(sigma - 1):
-                pixel_sums(sigma - 1, 3)

@@ -16,14 +16,14 @@ FLOPS = 2 * 4 * 64 * 256 * 12288
 
 P = 128
 PASS = 512
-STEP = 2 * PASS
 PIXELS = 12288
-PAIR_STEPS = PIXELS // STEP
-N_STEPS = 2 * PAIR_STEPS
-LEAD = 1
-AHEAD = 10
-FEATS_BLOCKS = [1] * 24
-PREDS_BLOCKS = [1] * 6 + [2] * 9
+PASSES = PIXELS // PASS
+UNIT = 4096
+WHOLE = [UNIT] * 3
+RAMP_UP = [512, 512, 1024, 2048, 2048, 2048, 4096]
+RAMP_DOWN = [4096, 4096, 2048, 1024, 512, 512]
+TILE_ORDER = [0, 2, 1, 3]
+RAW_BUFS = 14
 EPS = 1e-12
 
 
@@ -33,6 +33,26 @@ def tile_categoryalign_module_pa_kernel(tc, preds, feats, out):
     ff = feats.rearrange("b c h w -> (b c) (h w)")
     of = out.rearrange("b k c -> (b k) c")
 
+    units = []
+    for pair in range(2):
+        for j in [-1] + TILE_ORDER:
+            widths = WHOLE
+            if pair == 0 and j == -1:
+                widths = RAMP_UP
+            if pair == 1 and j == TILE_ORDER[-1]:
+                widths = RAMP_DOWN
+            px = 0
+            for width in widths:
+                units.append((pair, j, px, width))
+                px += width
+    n_units = len(units)
+    last_of = {}
+    for i in range(n_units):
+        last_of[units[i][0:2]] = i
+
+    def in_runs(a):
+        return 2 <= a < PASSES - 2
+
     with ExitStack() as ctx:
         const = ctx.enter_context(tc.tile_pool(name="const", bufs=1))
         raw_pool = ctx.enter_context(tc.tile_pool(name="raw_pool", bufs=1))
@@ -41,50 +61,20 @@ def tile_categoryalign_module_pa_kernel(tc, preds, feats, out):
         psum = ctx.enter_context(tc.psum_pool(name="psum", bufs=1))
         ctx.enter_context(tc.manual_schedule())
 
-        loads = []
-        first = 0
-        for width in PREDS_BLOCKS:
-            loads.append((first - LEAD, 0, width))
-            first += width
-        first = 0
-        for width in FEATS_BLOCKS:
-            loads.append((first, 1, width))
-            first += width
-        loads = sorted(loads)
-        preds_raw = {}
-        feats_raw = {}
+        raw = {}
 
-        def start_load(first_step, is_feats, arg):
-            if is_feats:
-                pair, local = divmod(first_step, PAIR_STEPS)
-                cols = STEP * arg
-                r = raw_pool.tile([P, 4 * STEP * max(FEATS_BLOCKS)], BF16, tag="rf", bufs=12, name="rf")
-                src = ff[4 * P * pair : 4 * P * (pair + 1), STEP * local : STEP * local + cols].rearrange(
-                    "(j p) x -> p j x", p=P
-                )
-                dst = r[:, 0 : 4 * cols].rearrange("p (j x) -> p j x", j=4)
-                if first_step == 0 or first_step + arg == N_STEPS:
-                    for j in range(4):
-                        nc.sync.dma_start(out=dst[:, j], in_=src[:, j])
-                else:
-                    nc.sync.dma_start(out=dst, in_=src)
-                for i in range(arg):
-                    feats_raw[first_step + i] = (r[:].bitcast(F32), (STEP // 2) * i, cols // 2)
+        def start_load(i):
+            pair, j, px, width = units[i]
+            r = raw_pool.tile([P, UNIT], BF16, tag="raw", bufs=RAW_BUFS, name="raw")
+            if j < 0:
+                src = pf[P * pair : P * pair + P, px : px + width]
             else:
-                sigma = first_step + LEAD
-                pair, local = divmod(sigma, PAIR_STEPS)
-                cols = STEP * arg
-                r = raw_pool.tile([P, STEP * max(PREDS_BLOCKS)], BF16, tag="rp", bufs=8, name="rp")
-                nc.sync.dma_start(
-                    out=r[:, 0:cols], in_=pf[P * pair : P * (pair + 1), STEP * local : STEP * local + cols]
-                )
-                for i in range(arg):
-                    preds_raw[sigma + i] = (r[:].bitcast(F32), (STEP // 2) * i)
+                src = ff[P * (4 * pair + j) : P * (4 * pair + j) + P, px : px + width]
+            nc.sync.dma_start(out=r[:, 0:width], in_=src)
+            raw[i] = r
 
-        n_started = 0
-        while n_started < len(loads) and loads[n_started][0] <= AHEAD - LEAD:
-            start_load(*loads[n_started])
-            n_started += 1
+        for i in range(RAW_BUFS):
+            start_load(i)
 
         ident = const.tile([P, P], F32, name="ident")
         make_identity(nc, ident[:])
@@ -106,114 +96,110 @@ def tile_categoryalign_module_pa_kernel(tc, preds, feats, out):
         nc.scalar.activation(out=table_warm[:], in_=one_col[:], func=ACT.Abs_reciprocal_sqrt)
 
         sums = psum.tile([P, 512], F32, tag="sums", name="sums")
-        preds_shuffled = {}
-        feats_shuffled = {}
-        preds_grouped = {}
-        feats_grouped = {}
-        preds_codes = {}
+        shuffled = {}
+        grouped = {}
         feats_codes = {}
+        preds_codes = {}
         acc = {}
         keep = {}
 
-        def live(x):
-            return 0 <= x < N_STEPS
+        def passes_of(i):
+            pair, j, px, width = units[i]
+            return list(range(px // PASS, (px + width) // PASS))
 
-        def shuffled(step):
-            return 2 <= step < N_STEPS - 1
-
-        def shuffle_preds(step):
-            words, word0 = preds_raw[step]
-            t = work.tile([P, PASS], BF16, tag="sp", bufs=3, name="sp")
-            raw = words.bitcast(BF16)[:, 2 * word0 + PASS : 2 * word0 + STEP]
+        def shuffle(i):
+            runs = [a for a in passes_of(i) if in_runs(a)]
+            if not runs:
+                return
+            px = units[i][2]
+            cols = PASS * len(runs)
+            t = work.tile([P, UNIT], BF16, tag="sh", bufs=3, name="sh")
+            first = PASS * runs[0] - px
             nc.vector.tensor_copy(
-                out=t[:].rearrange("p (u x e) -> p u x e", u=2, e=16),
-                in_=raw.rearrange("p (x u e) -> p u x e", u=2, e=16),
+                out=t[:, 0:cols].rearrange("p (u x e) -> p u x e", u=2, e=16),
+                in_=raw[i][:, first : first + cols].rearrange("p (x u e) -> p u x e", u=2, e=16),
             )
-            preds_shuffled[step] = t[:].bitcast(F32)
+            shuffled[i] = (t, runs)
 
-        def shuffle_feats(step):
-            words, word0, pitch = feats_raw[step]
-            t = work.tile([P, 4 * PASS], BF16, tag="sf", bufs=3, name="sf")
-            raw = words.bitcast(BF16)[:, 0 : 8 * pitch].rearrange("p (j c) -> p j c", j=4)
-            raw = raw[:, :, 2 * word0 + PASS : 2 * word0 + STEP].rearrange("p j (x u e) -> p u j x e", u=2, e=16)
-            dst = t[:].rearrange("p (u j x e) -> p u j x e", u=2, j=4, e=16)
-            for u in range(2):
-                nc.vector.tensor_copy(out=dst[:, u], in_=raw[:, u])
-            feats_shuffled[step] = t[:].bitcast(F32)
+        def windows(i, a):
+            if in_runs(a):
+                t, runs = shuffled[i]
+                k = a - runs[0]
+                return [t[:].bitcast(F32)[:, P * (len(runs) * u + k) : P * (len(runs) * u + k) + P] for u in range(2)]
+            w = 256 * (a - passes_of(i)[0])
+            return [raw[i][:].bitcast(F32)[:, w + u : w + 256 : 2] for u in range(2)]
 
-        def transpose_bank(windows, dst, copy):
-            bank = psum.tile([P, 512], F32, tag="bank", bufs=6, name="bank")
-            for a in range(2):
-                for u in range(2):
-                    k = 2 * a + u
-                    nc.tensor.transpose(bank[:, P * k : P * k + P], windows[a][u], ident[:])
-            copy(out=dst, in_=bank[:].rearrange("p (a u r) -> p a r u", a=2, u=2))
-
-        def every_second(words, word0):
-            return [words[:, word0 + u : word0 + 256 : 2] for u in range(2)]
-
-        def contiguous(words, word0, apart):
-            return [words[:, word0 + apart * u : word0 + apart * u + P] for u in range(2)]
-
-        def transpose_preds(sigma):
-            g = work.tile([P, 4 * 2 * P], BF16, tag="pg", bufs=3, name="pg", align_bytes=64)
-            preds_grouped[sigma] = g
-            words, word0 = preds_raw[sigma]
-            windows = [every_second(words, word0)]
-            if shuffled(sigma):
-                windows.append(contiguous(preds_shuffled[sigma], 0, PASS // 4))
-            else:
-                windows.append(every_second(words, word0 + 256))
-            transpose_bank(windows, g[:].bitcast(F32).rearrange("p (a r u) -> p a r u", a=2, u=2), nc.scalar.copy)
-
-        def transpose_feats(s, row_tiles):
-            if s not in feats_grouped:
-                feats_grouped[s] = work.tile([P, 4 * 2 * 4 * P], BF16, tag="fg", bufs=3, name="fg", align_bytes=64)
-            view = feats_grouped[s][:].bitcast(F32).rearrange("p (a j r u) -> p a j r u", a=2, j=4, u=2)
-            for j in row_tiles:
-                words, word0, pitch = feats_raw[s]
-                windows = [every_second(words, word0 + pitch * j)]
-                if shuffled(s):
-                    windows.append(contiguous(feats_shuffled[s], PASS // 4 * j, PASS))
-                else:
-                    windows.append(every_second(words, word0 + pitch * j + 256))
-                transpose_bank(windows, view[:, :, j], nc.vector.tensor_copy if j == 3 else nc.scalar.copy)
-
-        def quantise(grouped, tag, bufs):
-            width = grouped.shape[1] // 4
-            codes = work.tile([P, width], U32, tag=tag + "c", bufs=bufs, name=tag + "c", align_bytes=64)
-            scales = work.tile([P, width], U8, tag=tag + "s", bufs=bufs, name=tag + "s", align_bytes=64)
-            nc.vector.quantize_mx(out=codes[:].bitcast(FP8X4), scales=scales[:], in_=grouped[:])
-            return codes, scales
-
-        def pixel_sums(sigma, quarter):
-            pair, local = divmod(sigma, PAIR_STEPS)
-            a, half = divmod(quarter, 2)
-            for j in (2 * half, 2 * half + 1):
-                col = 96 * pair + 24 * j + 2 * local + a
-                nc.tensor.matmul(
-                    out=sums[:, col : col + 1],
-                    lhsT=preds_grouped[sigma][:, 512 * a + P * j : 512 * a + P * j + P],
-                    rhs=ones[:, 0:1],
-                    start=True,
-                    stop=True,
+        def transpose_unit(i):
+            passes = passes_of(i)
+            n = len(passes)
+            g = work.tile([P, UNIT], BF16, tag="grouped", bufs=3, name="grouped", align_bytes=64)
+            grouped[i] = g
+            view = g[:, 0 : PASS * n].bitcast(F32).rearrange("p (a r u) -> p a r u", r=P, u=2)
+            for b in range(0, n, 2):
+                m = min(2, n - b)
+                bank = psum.tile([P, 512], F32, tag="bank", bufs=6, name="bank")
+                for k in range(m):
+                    w = windows(i, passes[b + k])
+                    for u in range(2):
+                        c = P * (2 * k + u)
+                        nc.tensor.transpose(bank[:, c : c + P], w[u], ident[:])
+                by_vector = n < 8 and b % 4 == 2
+                copy = nc.vector.tensor_copy if by_vector else nc.scalar.copy
+                copy(
+                    out=view[:, b : b + m],
+                    in_=bank[:, 0 : 256 * m].rearrange("p (a u r) -> p a r u", u=2, r=P),
                 )
 
-        def mx_pass(s, a):
-            pair, local = divmod(s, PAIR_STEPS)
-            if local == 0 and a == 0:
-                acc[pair] = psum.tile([P, 512], F32, tag="acc", name="acc")
-            pc, ps = preds_codes[s]
-            fc, fs = feats_codes[s]
-            nc.tensor.matmul_mx(
-                out=acc[pair][:],
-                lhsT=pc[:, P * a : P * a + P].bitcast(FP8X4),
-                lhsT_scale=ps[:, P * a : P * a + P],
-                rhs=fc[:, 512 * a : 512 * a + 512].bitcast(FP8X4),
-                rhs_scale=fs[:, 512 * a : 512 * a + 512],
-                start=(local == 0 and a == 0),
-                stop=(local == PAIR_STEPS - 1 and a == 1),
-            )
+        def quantise(i):
+            pair, j, px, width = units[i]
+            if j < 0:
+                if px == 0:
+                    preds_codes[pair] = (
+                        work.tile([P, P * PASSES], U32, tag="pc", bufs=2, name="pc", align_bytes=64),
+                        work.tile([P, P * PASSES], U8, tag="ps", bufs=2, name="ps", align_bytes=64),
+                    )
+                codes, scales = preds_codes[pair]
+                c0 = px // 4
+            else:
+                codes = work.tile([P, UNIT // 4], U32, tag="fc", bufs=4, name="fc", align_bytes=64)
+                scales = work.tile([P, UNIT // 4], U8, tag="fs", bufs=4, name="fs", align_bytes=64)
+                feats_codes[i] = (codes, scales)
+                c0 = 0
+            cols = slice(c0, c0 + width // 4)
+            nc.vector.quantize_mx(out=codes[:, cols].bitcast(FP8X4), scales=scales[:, cols], in_=grouped[i][:, 0:width])
+
+        def pixel_sums(i):
+            pair = units[i][0]
+            passes = passes_of(i)
+            for k in range(len(passes)):
+                for j in range(4):
+                    col = 96 * pair + 24 * j + passes[k]
+                    nc.tensor.matmul(
+                        out=sums[:, col : col + 1],
+                        lhsT=grouped[i][:, PASS * k + P * j : PASS * k + P * j + P],
+                        rhs=ones[:, 0:1],
+                        start=True,
+                        stop=True,
+                    )
+
+        def mx_unit(i):
+            pair, j, px, width = units[i]
+            if px == 0:
+                acc[(pair, j)] = psum.tile([P, P], F32, tag="acc", name="acc")
+            pc, ps = preds_codes[pair]
+            fc, fs = feats_codes[i]
+            passes = passes_of(i)
+            for k in range(len(passes)):
+                a = passes[k]
+                nc.tensor.matmul_mx(
+                    out=acc[(pair, j)][:],
+                    lhsT=pc[:, P * a : P * a + P].bitcast(FP8X4),
+                    lhsT_scale=ps[:, P * a : P * a + P],
+                    rhs=fc[:, P * k : P * k + P].bitcast(FP8X4),
+                    rhs_scale=fs[:, P * k : P * k + P],
+                    start=(a == 0),
+                    stop=(a == PASSES - 1),
+                )
 
         def denominator_fold(pair):
             part = tail.tile([P, 4], F32, tag="part", name="part")
@@ -240,98 +226,94 @@ def tile_categoryalign_module_pa_kernel(tc, preds, feats, out):
             nc.vector.reciprocal(out=rd[:], in_=sums[:, 192 + pair : 193 + pair])
             keep[("rd", pair)] = rd
 
-        def finish_square(pair):
+        def read_sums(pair, j):
             rd = keep[("rd", pair)]
-            sq = tail.tile([P, 256], F32, tag="sq", name="sq")
-            vec = tail.tile([P, 256], F32, tag="vec", name="vec")
-            keep[("sq", pair)] = sq
-            keep[("vec", pair)] = vec
-            for h in range(2):
-                rows = slice(64 * h, 64 * h + 64)
-                cols = slice(256 * h, 256 * h + 256)
-                if pair == 0:
-                    nc.scalar.activation(out=vec[rows, :], in_=acc[pair][rows, cols], func=ACT.Copy, scale=rd[rows, 0:1])
-                else:
-                    nc.scalar.activation(
-                        out=sq[rows, :], in_=acc[pair][rows, cols], func=ACT.Square, scale=rd[rows, 0:1]
-                    )
-            if pair == 1:
-                for h in range(2):
-                    rows = slice(64 * h, 64 * h + 64)
-                    cols = slice(256 * h, 256 * h + 256)
-                    nc.vector.tensor_scalar_mul(out=vec[rows, :], in0=acc[pair][rows, cols], scalar1=rd[rows, 0:1])
+            half = j % 2
+            if ("vec", pair, half) not in keep:
+                keep[("vec", pair, half)] = tail.tile([P, P], F32, tag="vec", name="vec")
+                keep[("sq", pair, half)] = tail.tile([P, P], F32, tag="sq", name="sq")
+            rows = slice(64 * (j // 2), 64 * (j // 2) + 64)
+            vec = keep[("vec", pair, half)][rows, :]
+            if last_of[(pair, j)] == n_units - 1:
+                sq = keep[("sq", pair, half)][rows, :]
+                nc.scalar.activation(out=sq, in_=acc[(pair, j)][rows, :], func=ACT.Square, scale=rd[rows, 0:1])
+                nc.vector.tensor_scalar_mul(out=vec, in0=acc[(pair, j)][rows, :], scalar1=rd[rows, 0:1])
+            else:
+                nc.scalar.activation(out=vec, in_=acc[(pair, j)][rows, :], func=ACT.Copy, scale=rd[rows, 0:1])
 
-        def finish_square_of_vec(pair):
-            vec = keep[("vec", pair)]
-            nc.vector.tensor_tensor(out=keep[("sq", pair)][:], in0=vec[:], in1=vec[:], op=ALU.mult)
+        def square(pair, j):
+            if last_of[(pair, j)] == n_units - 1:
+                return
+            rows = slice(64 * (j // 2), 64 * (j // 2) + 64)
+            vec = keep[("vec", pair, j % 2)][rows, :]
+            nc.vector.tensor_tensor(out=keep[("sq", pair, j % 2)][rows, :], in0=vec, in1=vec, op=ALU.mult)
 
-        def finish_norm(pair):
+        def finish_norm(pair, half):
             bank = psum.tile([P, 512], F32, tag="bank", bufs=6, name="bank")
-            nc.tensor.matmul(out=bank[:, 0:256], lhsT=same_image[:], rhs=keep[("sq", pair)][:], start=True, stop=True)
-            keep[("nsq", pair)] = bank
+            nc.tensor.matmul(out=bank[:, 0:P], lhsT=same_image[:], rhs=keep[("sq", pair, half)][:], start=True, stop=True)
+            keep[("nsq", pair, half)] = bank
 
-        def finish_root(pair):
-            rn = tail.tile([P, 256], F32, tag="rn", name="rn")
-            nc.scalar.activation(out=rn[:], in_=keep[("nsq", pair)][:, 0:256], func=ACT.Abs_reciprocal_sqrt)
-            keep[("rn", pair)] = rn
+        def finish_root(pair, half):
+            rn = tail.tile([P, P], F32, tag="rn", name="rn")
+            nc.scalar.activation(out=rn[:], in_=keep[("nsq", pair, half)][:, 0:P], func=ACT.Abs_reciprocal_sqrt)
+            keep[("rn", pair, half)] = rn
 
-        def finish_store(pair):
-            res = tail.tile([P, 256], F32, tag="res", name="res")
+        def finish_divide(pair, half):
+            res = tail.tile([P, P], F32, tag="res", name="res")
             nc.vector.scalar_tensor_tensor(
                 out=res[:],
-                in0=keep[("rn", pair)][:],
+                in0=keep[("rn", pair, half)][:],
                 scalar=1.0 / EPS,
-                in1=keep[("vec", pair)][:],
+                in1=keep[("vec", pair, half)][:],
                 op0=ALU.min,
                 op1=ALU.mult,
             )
-            nc.sync.dma_start(out=of[P * pair : P * pair + P, :], in_=res[:])
+            keep[("res", pair, half)] = res
 
-        for s in range(-LEAD, N_STEPS + 6):
-            sigma = s + LEAD
+        def finish_store(pair, half):
+            nc.sync.dma_start(
+                out=of[P * pair : P * pair + P, P * half : P * half + P], in_=keep[("res", pair, half)][:]
+            )
+
+        def live(i):
+            return 0 <= i < n_units
+
+        for i in range(-1, n_units + 7):
             for pair in range(2):
-                summed = PAIR_STEPS * (pair + 1) - LEAD
-                closed = PAIR_STEPS * (pair + 1) + 1
-                if s == summed + 1:
+                end = last_of[(pair, -1)]
+                if i == end + 2:
                     denominator_fold(pair)
-                if s == summed + 2:
+                if i == end + 3:
                     denominator_invert(pair)
-                if s == closed + 1:
-                    finish_square(pair)
-                late = 1 - pair
-                if pair == 0 and s == closed + 2:
-                    finish_square_of_vec(pair)
-                if s == closed + 2 + late:
-                    finish_root(pair)
-                if s == closed + 3 + late:
-                    finish_store(pair)
-            if live(s + 1) and shuffled(s + 1):
-                shuffle_feats(s + 1)
-            if live(sigma + 1) and shuffled(sigma + 1):
-                shuffle_preds(sigma + 1)
-            if live(sigma - 1):
-                preds_codes[sigma - 1] = quantise(preds_grouped[sigma - 1], "p", 8)
-            if live(s - 1):
-                feats_codes[s - 1] = quantise(feats_grouped[s - 1], "f", 4)
-            if live(sigma):
-                transpose_preds(sigma)
-            if live(s):
-                transpose_feats(s, (0, 1, 2, 3))
-            while n_started < len(loads) and loads[n_started][0] <= s + AHEAD:
-                start_load(*loads[n_started])
-                n_started += 1
-            opens = s - 2 == PAIR_STEPS
-            if live(s - 2) and not opens:
-                mx_pass(s - 2, 0)
-            if live(sigma - 1):
-                for quarter in range(4):
-                    pixel_sums(sigma - 1, quarter)
-            if live(s - 2):
-                if opens:
-                    mx_pass(s - 2, 0)
-                mx_pass(s - 2, 1)
+                for j in TILE_ORDER:
+                    end = last_of[(pair, j)]
+                    if i == end + 3:
+                        read_sums(pair, j)
+                    if i == end + 4:
+                        square(pair, j)
+                    if j >= 2:
+                        if i == end + 5:
+                            finish_root(pair, j % 2)
+                        if i == end + 6:
+                            finish_divide(pair, j % 2)
+            if live(i + 1):
+                shuffle(i + 1)
+            if live(i - 1):
+                quantise(i - 1)
+            if live(i):
+                transpose_unit(i)
+                if i + RAW_BUFS < n_units:
+                    start_load(i + RAW_BUFS)
+            if live(i - 1) and units[i - 1][1] < 0:
+                pixel_sums(i - 1)
+            if live(i - 2) and units[i - 2][1] >= 0:
+                mx_unit(i - 2)
             for pair in range(2):
-                if s == PAIR_STEPS * (pair + 1) - LEAD + 1:
+                if i == last_of[(pair, -1)] + 2:
                     denominator_place(pair)
-                if s == PAIR_STEPS * (pair + 1) + 3 - pair:
-                    finish_norm(pair)
+                for j in (2, 3):
+                    end = last_of[(pair, j)]
+                    if i == end + 4:
+                        finish_norm(pair, j % 2)
+                    if i == end + 6:
+                        finish_store(pair, j % 2)

@@ -21,9 +21,9 @@ PASSES = PIXELS // PASS
 UNIT = 4096
 WHOLE = [UNIT] * 3
 RAMP_UP = [512, 512, 1024, 2048, 2048, 2048, 4096]
-RAMP_DOWN = [4096, 4096, 2048, 1024, 512, 512]
+RAMP_DOWN = [4096, 4096, 2048, 1024, 1024]
 TILE_ORDER = [0, 2, 1, 3]
-RAW_BUFS = 14
+RAW_BUFS = 11
 EPS = 1e-12
 
 
@@ -51,7 +51,7 @@ def tile_categoryalign_module_pa_kernel(tc, preds, feats, out):
         last_of[units[i][0:2]] = i
 
     def in_runs(a):
-        return 2 <= a < PASSES - 2
+        return a % 8 >= 3
 
     with ExitStack() as ctx:
         const = ctx.enter_context(tc.tile_pool(name="const", bufs=1))
@@ -132,7 +132,7 @@ def tile_categoryalign_module_pa_kernel(tc, preds, feats, out):
         def transpose_unit(i):
             passes = passes_of(i)
             n = len(passes)
-            g = work.tile([P, UNIT], BF16, tag="grouped", bufs=3, name="grouped", align_bytes=64)
+            g = work.tile([P, UNIT], BF16, tag="grouped", bufs=5, name="grouped", align_bytes=64)
             grouped[i] = g
             view = g[:, 0 : PASS * n].bitcast(F32).rearrange("p (a r u) -> p a r u", r=P, u=2)
             for b in range(0, n, 2):
@@ -143,7 +143,7 @@ def tile_categoryalign_module_pa_kernel(tc, preds, feats, out):
                     for u in range(2):
                         c = P * (2 * k + u)
                         nc.tensor.transpose(bank[:, c : c + P], w[u], ident[:])
-                by_vector = n < 8 and b % 4 == 2
+                by_vector = b % 4 == 2 if n < 8 else b == 4 and i % 2 == 0
                 copy = nc.vector.tensor_copy if by_vector else nc.scalar.copy
                 copy(
                     out=view[:, b : b + m],
@@ -161,8 +161,8 @@ def tile_categoryalign_module_pa_kernel(tc, preds, feats, out):
                 codes, scales = preds_codes[pair]
                 c0 = px // 4
             else:
-                codes = work.tile([P, UNIT // 4], U32, tag="fc", bufs=4, name="fc", align_bytes=64)
-                scales = work.tile([P, UNIT // 4], U8, tag="fs", bufs=4, name="fs", align_bytes=64)
+                codes = work.tile([P, UNIT // 4], U32, tag="fc", bufs=6, name="fc", align_bytes=64)
+                scales = work.tile([P, UNIT // 4], U8, tag="fs", bufs=6, name="fs", align_bytes=64)
                 feats_codes[i] = (codes, scales)
                 c0 = 0
             cols = slice(c0, c0 + width // 4)
@@ -278,42 +278,49 @@ def tile_categoryalign_module_pa_kernel(tc, preds, feats, out):
         def live(i):
             return 0 <= i < n_units
 
-        for i in range(-1, n_units + 7):
+        pending = []
+        for i in range(-1, n_units + 9):
             for pair in range(2):
                 end = last_of[(pair, -1)]
-                if i == end + 2:
-                    denominator_fold(pair)
                 if i == end + 3:
+                    denominator_fold(pair)
+                if i == end + 4:
                     denominator_invert(pair)
                 for j in TILE_ORDER:
                     end = last_of[(pair, j)]
-                    if i == end + 3:
+                    if i == end + 5:
                         read_sums(pair, j)
-                    if i == end + 4:
+                    if i == end + 6:
                         square(pair, j)
                     if j >= 2:
-                        if i == end + 5:
+                        if i == end + 7:
                             finish_root(pair, j % 2)
-                        if i == end + 6:
+                        if i == end + 8:
                             finish_divide(pair, j % 2)
             if live(i + 1):
                 shuffle(i + 1)
-            if live(i - 1):
-                quantise(i - 1)
+            if live(i - 2):
+                quantise(i - 2)
             if live(i):
                 transpose_unit(i)
                 if i + RAW_BUFS < n_units:
                     start_load(i + RAW_BUFS)
-            if live(i - 1) and units[i - 1][1] < 0:
-                pixel_sums(i - 1)
-            if live(i - 2) and units[i - 2][1] >= 0:
-                mx_unit(i - 2)
+            if live(i - 2) and units[i - 2][1] < 0:
+                pixel_sums(i - 2)
+            m = i - 4
+            if live(m) and units[m][1] >= 0:
+                pending.append(m)
+                ramp = units[m][0:2] == (1, TILE_ORDER[-1])
+                if len(pending) == 2 or ramp or m == last_of[units[m][0:2]]:
+                    for unit in pending:
+                        mx_unit(unit)
+                    pending.clear()
             for pair in range(2):
-                if i == last_of[(pair, -1)] + 2:
+                if i == last_of[(pair, -1)] + 3:
                     denominator_place(pair)
                 for j in (2, 3):
                     end = last_of[(pair, j)]
-                    if i == end + 4:
-                        finish_norm(pair, j % 2)
                     if i == end + 6:
+                        finish_norm(pair, j % 2)
+                    if i == end + 8:
                         finish_store(pair, j % 2)

@@ -20,10 +20,13 @@ PIXELS = 12288
 PASSES = PIXELS // PASS
 UNIT = 4096
 WHOLE = [UNIT] * 3
-RAMP_UP = [512, 512, 1024, 2048, 2048, 2048, 4096]
+RAMP_UP = [1024, 1024, 2048, 4096, 4096]
 RAMP_DOWN = [4096, 4096, 2048, 1024, 1024]
 TILE_ORDER = [0, 2, 1, 3]
 RAW_BUFS = 11
+QUANTISE = 2
+MULTIPLY = 3
+EQUAL_COLUMNS = 20
 EPS = 1e-12
 
 
@@ -33,25 +36,27 @@ def tile_categoryalign_module_pa_kernel(tc, preds, feats, out):
     ff = feats.rearrange("b c h w -> (b c) (h w)")
     of = out.rearrange("b k c -> (b k) c")
 
-    units = []
-    for pair in range(2):
-        for j in [-1] + TILE_ORDER:
-            widths = WHOLE
-            if pair == 0 and j == -1:
-                widths = RAMP_UP
-            if pair == 1 and j == TILE_ORDER[-1]:
-                widths = RAMP_DOWN
-            px = 0
-            for width in widths:
-                units.append((pair, j, px, width))
-                px += width
+    def cut(pair, j, widths):
+        px = 0
+        cuts = []
+        for width in widths:
+            cuts.append((pair, j, px, width))
+            px += width
+        return cuts
+
+    def woven(a, b):
+        return [unit for both in zip(a, b) for unit in both]
+
+    units = woven(cut(0, -1, RAMP_UP), cut(0, 0, RAMP_UP)) + cut(0, 2, WHOLE) + cut(0, 1, WHOLE)
+    units += woven(cut(0, 3, WHOLE), cut(1, -1, WHOLE))
+    units += cut(1, 0, WHOLE) + cut(1, 2, WHOLE) + cut(1, 1, WHOLE) + cut(1, 3, RAMP_DOWN)
     n_units = len(units)
     last_of = {}
     for i in range(n_units):
         last_of[units[i][0:2]] = i
 
     def in_runs(a):
-        return a % 8 >= 3
+        return a % 8 >= 2
 
     with ExitStack() as ctx:
         const = ctx.enter_context(tc.tile_pool(name="const", bufs=1))
@@ -78,7 +83,7 @@ def tile_categoryalign_module_pa_kernel(tc, preds, feats, out):
 
         ident = const.tile([P, P], F32, name="ident")
         make_identity(nc, ident[:])
-        ones = const.tile([P, 2], BF16, name="ones")
+        ones = const.tile([P, EQUAL_COLUMNS], BF16, name="ones")
         nc.vector.memset(ones[:], 1.0)
         fold = const.tile([P, 32], F32, name="fold")
         nc.vector.tensor_reduce(out=fold[:], in_=ident[:].rearrange("p (a t) -> p a t", t=4), axis=AX.X, op=ALU.add)
@@ -143,7 +148,7 @@ def tile_categoryalign_module_pa_kernel(tc, preds, feats, out):
                     for u in range(2):
                         c = P * (2 * k + u)
                         nc.tensor.transpose(bank[:, c : c + P], w[u], ident[:])
-                by_vector = b % 4 == 2 if n < 8 else b == 4 and i % 2 == 0
+                by_vector = b % 4 == 2 if n < 8 else b == 6 and i % 5 == 0
                 copy = nc.vector.tensor_copy if by_vector else nc.scalar.copy
                 copy(
                     out=view[:, b : b + m],
@@ -173,11 +178,11 @@ def tile_categoryalign_module_pa_kernel(tc, preds, feats, out):
             passes = passes_of(i)
             for k in range(len(passes)):
                 for j in range(4):
-                    col = 96 * pair + 24 * j + passes[k]
+                    col = 256 * pair + 4 * passes[k] + j
                     nc.tensor.matmul(
-                        out=sums[:, col : col + 1],
+                        out=sums[:, col : col + EQUAL_COLUMNS],
                         lhsT=grouped[i][:, PASS * k + P * j : PASS * k + P * j + P],
-                        rhs=ones[:, 0:1],
+                        rhs=ones[:],
                         start=True,
                         stop=True,
                     )
@@ -205,7 +210,7 @@ def tile_categoryalign_module_pa_kernel(tc, preds, feats, out):
             part = tail.tile([P, 4], F32, tag="part", name="part")
             nc.vector.tensor_reduce(
                 out=part[:],
-                in_=sums[:, 96 * pair : 96 * pair + 96].rearrange("p (j x) -> p j x", j=4),
+                in_=sums[:, 256 * pair : 256 * pair + 96].rearrange("p (x j) -> p j x", j=4),
                 axis=AX.X,
                 op=ALU.add,
             )
@@ -214,7 +219,7 @@ def tile_categoryalign_module_pa_kernel(tc, preds, feats, out):
         def denominator_place(pair):
             for j in range(4):
                 nc.tensor.matmul(
-                    out=sums[:, 192 + pair : 193 + pair],
+                    out=sums[:, 128 + 256 * pair : 129 + 256 * pair],
                     lhsT=sel[:, P * j : P * j + P],
                     rhs=keep[("part", pair)][:, j : j + 1],
                     start=(j == 0),
@@ -223,7 +228,7 @@ def tile_categoryalign_module_pa_kernel(tc, preds, feats, out):
 
         def denominator_invert(pair):
             rd = tail.tile([P, 1], F32, tag="rd", name="rd")
-            nc.vector.reciprocal(out=rd[:], in_=sums[:, 192 + pair : 193 + pair])
+            nc.vector.reciprocal(out=rd[:], in_=sums[:, 128 + 256 * pair : 129 + 256 * pair])
             keep[("rd", pair)] = rd
 
         def read_sums(pair, j):
@@ -278,7 +283,6 @@ def tile_categoryalign_module_pa_kernel(tc, preds, feats, out):
         def live(i):
             return 0 <= i < n_units
 
-        pending = []
         for i in range(-1, n_units + 9):
             for pair in range(2):
                 end = last_of[(pair, -1)]
@@ -288,39 +292,33 @@ def tile_categoryalign_module_pa_kernel(tc, preds, feats, out):
                     denominator_invert(pair)
                 for j in TILE_ORDER:
                     end = last_of[(pair, j)]
-                    if i == end + 5:
+                    if i == end + 1 + MULTIPLY:
                         read_sums(pair, j)
-                    if i == end + 6:
+                    if i == end + 2 + MULTIPLY:
                         square(pair, j)
                     if j >= 2:
-                        if i == end + 7:
+                        if i == end + 3 + MULTIPLY:
                             finish_root(pair, j % 2)
-                        if i == end + 8:
+                        if i == end + 4 + MULTIPLY:
                             finish_divide(pair, j % 2)
             if live(i + 1):
                 shuffle(i + 1)
-            if live(i - 2):
-                quantise(i - 2)
+            if live(i - QUANTISE):
+                quantise(i - QUANTISE)
             if live(i):
                 transpose_unit(i)
                 if i + RAW_BUFS < n_units:
                     start_load(i + RAW_BUFS)
-            if live(i - 2) and units[i - 2][1] < 0:
-                pixel_sums(i - 2)
-            m = i - 4
-            if live(m) and units[m][1] >= 0:
-                pending.append(m)
-                ramp = units[m][0:2] == (1, TILE_ORDER[-1])
-                if len(pending) == 2 or ramp or m == last_of[units[m][0:2]]:
-                    for unit in pending:
-                        mx_unit(unit)
-                    pending.clear()
+            if live(i - QUANTISE) and units[i - QUANTISE][1] < 0:
+                pixel_sums(i - QUANTISE)
+            if live(i - MULTIPLY) and units[i - MULTIPLY][1] >= 0:
+                mx_unit(i - MULTIPLY)
             for pair in range(2):
                 if i == last_of[(pair, -1)] + 3:
                     denominator_place(pair)
                 for j in (2, 3):
                     end = last_of[(pair, j)]
-                    if i == end + 6:
+                    if i == end + 2 + MULTIPLY:
                         finish_norm(pair, j % 2)
-                    if i == end + 8:
+                    if i == end + 4 + MULTIPLY:
                         finish_store(pair, j % 2)

from contextlib import ExitStack

import concourse.mybir as mybir
from concourse.masks import make_identity

F32 = mybir.dt.float32
BF16 = mybir.dt.bfloat16
U32 = mybir.dt.uint32
U8 = mybir.dt.uint8
FP8X4 = mybir.dt.float8_e4m3fn_x4
ALU = mybir.AluOpType
ACT = mybir.ActivationFunctionType
AX = mybir.AxisListType

FLOPS = 2 * 4 * 64 * 256 * 12288

P = 128
PASS = 512
PIXELS = 12288
PASSES = PIXELS // PASS
UNIT = 4096
WHOLE = [UNIT] * 3
RAMP_UP = [1024, 1024, 2048, 4096, 4096]
RAMP_DOWN = [4096, 4096, 2048, 1024, 1024]
TILE_ORDER = [0, 2, 1, 3]
RAW_BUFS = 11
QUANTISE = 2
MULTIPLY = 3
EQUAL_COLUMNS = 20
EPS = 1e-12


def tile_categoryalign_module_pa_kernel(tc, preds, feats, out):
    nc = tc.nc
    pf = preds.rearrange("b k h w -> (b k) (h w)")
    ff = feats.rearrange("b c h w -> (b c) (h w)")
    of = out.rearrange("b k c -> (b k) c")

    def cut(pair, j, widths):
        px = 0
        cuts = []
        for width in widths:
            cuts.append((pair, j, px, width))
            px += width
        return cuts

    def woven(a, b):
        return [unit for both in zip(a, b) for unit in both]

    units = woven(cut(0, -1, RAMP_UP), cut(0, 0, RAMP_UP)) + cut(0, 2, WHOLE) + cut(0, 1, WHOLE)
    units += woven(cut(0, 3, WHOLE), cut(1, -1, WHOLE))
    units += cut(1, 0, WHOLE) + cut(1, 2, WHOLE) + cut(1, 1, WHOLE) + cut(1, 3, RAMP_DOWN)
    n_units = len(units)
    last_of = {}
    for i in range(n_units):
        last_of[units[i][0:2]] = i

    def in_runs(a):
        return a % 8 >= 2

    with ExitStack() as ctx:
        const = ctx.enter_context(tc.tile_pool(name="const", bufs=1))
        raw_pool = ctx.enter_context(tc.tile_pool(name="raw_pool", bufs=1))
        work = ctx.enter_context(tc.tile_pool(name="work", bufs=1))
        tail = ctx.enter_context(tc.tile_pool(name="tail", bufs=2))
        psum = ctx.enter_context(tc.psum_pool(name="psum", bufs=1))
        ctx.enter_context(tc.manual_schedule())

        raw = {}

        def start_load(i):
            pair, j, px, width = units[i]
            r = raw_pool.tile([P, UNIT], BF16, tag="raw", bufs=RAW_BUFS, name="raw")
            if j < 0:
                src = pf[P * pair : P * pair + P, px : px + width]
            else:
                src = ff[P * (4 * pair + j) : P * (4 * pair + j) + P, px : px + width]
            nc.sync.dma_start(out=r[:, 0:width], in_=src)
            raw[i] = r

        for i in range(RAW_BUFS):
            start_load(i)

        ident = const.tile([P, P], F32, name="ident")
        make_identity(nc, ident[:])
        ones = const.tile([P, EQUAL_COLUMNS], BF16, name="ones")
        nc.vector.memset(ones[:], 1.0)
        fold = const.tile([P, 32], F32, name="fold")
        nc.vector.tensor_reduce(out=fold[:], in_=ident[:].rearrange("p (a t) -> p a t", t=4), axis=AX.X, op=ALU.add)
        sel = const.tile([P, 4 * P], F32, name="sel")
        nc.vector.memset(sel[:], 0.0)
        for j in range(4):
            nc.vector.tensor_copy(out=sel[:, (P + 32) * j : (P + 32) * j + 32], in_=fold[:])
        same_image = const.tile([P, P], F32, name="same_image")
        nc.vector.memset(same_image[:], 0.0)
        nc.vector.memset(same_image[0:64, 0:64], 1.0)
        nc.vector.memset(same_image[64:128, 64:128], 1.0)
        one_col = const.tile([P, 1], F32, name="one_col")
        nc.vector.memset(one_col[:], 1.0)
        table_warm = const.tile([P, 1], F32, name="table_warm")
        nc.scalar.activation(out=table_warm[:], in_=one_col[:], func=ACT.Abs_reciprocal_sqrt)

        sums = psum.tile([P, 512], F32, tag="sums", name="sums")
        shuffled = {}
        grouped = {}
        feats_codes = {}
        preds_codes = {}
        acc = {}
        keep = {}

        def passes_of(i):
            pair, j, px, width = units[i]
            return list(range(px // PASS, (px + width) // PASS))

        def shuffle(i):
            runs = [a for a in passes_of(i) if in_runs(a)]
            if not runs:
                return
            px = units[i][2]
            cols = PASS * len(runs)
            t = work.tile([P, UNIT], BF16, tag="sh", bufs=3, name="sh")
            first = PASS * runs[0] - px
            nc.vector.tensor_copy(
                out=t[:, 0:cols].rearrange("p (u x e) -> p u x e", u=2, e=16),
                in_=raw[i][:, first : first + cols].rearrange("p (x u e) -> p u x e", u=2, e=16),
            )
            shuffled[i] = (t, runs)

        def windows(i, a):
            if in_runs(a):
                t, runs = shuffled[i]
                k = a - runs[0]
                return [t[:].bitcast(F32)[:, P * (len(runs) * u + k) : P * (len(runs) * u + k) + P] for u in range(2)]
            w = 256 * (a - passes_of(i)[0])
            return [raw[i][:].bitcast(F32)[:, w + u : w + 256 : 2] for u in range(2)]

        def transpose_unit(i):
            passes = passes_of(i)
            n = len(passes)
            g = work.tile([P, UNIT], BF16, tag="grouped", bufs=5, name="grouped", align_bytes=64)
            grouped[i] = g
            view = g[:, 0 : PASS * n].bitcast(F32).rearrange("p (a r u) -> p a r u", r=P, u=2)
            for b in range(0, n, 2):
                m = min(2, n - b)
                bank = psum.tile([P, 512], F32, tag="bank", bufs=6, name="bank")
                for k in range(m):
                    w = windows(i, passes[b + k])
                    for u in range(2):
                        c = P * (2 * k + u)
                        nc.tensor.transpose(bank[:, c : c + P], w[u], ident[:])
                by_vector = b % 4 == 2 if n < 8 else b == 6 and i % 5 == 0
                copy = nc.vector.tensor_copy if by_vector else nc.scalar.copy
                copy(
                    out=view[:, b : b + m],
                    in_=bank[:, 0 : 256 * m].rearrange("p (a u r) -> p a r u", u=2, r=P),
                )

        def quantise(i):
            pair, j, px, width = units[i]
            if j < 0:
                if px == 0:
                    preds_codes[pair] = (
                        work.tile([P, P * PASSES], U32, tag="pc", bufs=2, name="pc", align_bytes=64),
                        work.tile([P, P * PASSES], U8, tag="ps", bufs=2, name="ps", align_bytes=64),
                    )
                codes, scales = preds_codes[pair]
                c0 = px // 4
            else:
                codes = work.tile([P, UNIT // 4], U32, tag="fc", bufs=6, name="fc", align_bytes=64)
                scales = work.tile([P, UNIT // 4], U8, tag="fs", bufs=6, name="fs", align_bytes=64)
                feats_codes[i] = (codes, scales)
                c0 = 0
            cols = slice(c0, c0 + width // 4)
            nc.vector.quantize_mx(out=codes[:, cols].bitcast(FP8X4), scales=scales[:, cols], in_=grouped[i][:, 0:width])

        def pixel_sums(i):
            pair = units[i][0]
            passes = passes_of(i)
            for k in range(len(passes)):
                for j in range(4):
                    col = 256 * pair + 4 * passes[k] + j
                    nc.tensor.matmul(
                        out=sums[:, col : col + EQUAL_COLUMNS],
                        lhsT=grouped[i][:, PASS * k + P * j : PASS * k + P * j + P],
                        rhs=ones[:],
                        start=True,
                        stop=True,
                    )

        def mx_unit(i):
            pair, j, px, width = units[i]
            if px == 0:
                acc[(pair, j)] = psum.tile([P, P], F32, tag="acc", name="acc")
            pc, ps = preds_codes[pair]
            fc, fs = feats_codes[i]
            passes = passes_of(i)
            for k in range(len(passes)):
                a = passes[k]
                nc.tensor.matmul_mx(
                    out=acc[(pair, j)][:],
                    lhsT=pc[:, P * a : P * a + P].bitcast(FP8X4),
                    lhsT_scale=ps[:, P * a : P * a + P],
                    rhs=fc[:, P * k : P * k + P].bitcast(FP8X4),
                    rhs_scale=fs[:, P * k : P * k + P],
                    start=(a == 0),
                    stop=(a == PASSES - 1),
                )

        def denominator_fold(pair):
            part = tail.tile([P, 4], F32, tag="part", name="part")
            nc.vector.tensor_reduce(
                out=part[:],
                in_=sums[:, 256 * pair : 256 * pair + 96].rearrange("p (x j) -> p j x", j=4),
                axis=AX.X,
                op=ALU.add,
            )
            keep[("part", pair)] = part

        def denominator_place(pair):
            for j in range(4):
                nc.tensor.matmul(
                    out=sums[:, 128 + 256 * pair : 129 + 256 * pair],
                    lhsT=sel[:, P * j : P * j + P],
                    rhs=keep[("part", pair)][:, j : j + 1],
                    start=(j == 0),
                    stop=(j == 3),
                )

        def denominator_invert(pair):
            rd = tail.tile([P, 1], F32, tag="rd", name="rd")
            nc.vector.reciprocal(out=rd[:], in_=sums[:, 128 + 256 * pair : 129 + 256 * pair])
            keep[("rd", pair)] = rd

        def read_sums(pair, j):
            rd = keep[("rd", pair)]
            half = j % 2
            if ("vec", pair, half) not in keep:
                keep[("vec", pair, half)] = tail.tile([P, P], F32, tag="vec", name="vec")
                keep[("sq", pair, half)] = tail.tile([P, P], F32, tag="sq", name="sq")
            rows = slice(64 * (j // 2), 64 * (j // 2) + 64)
            vec = keep[("vec", pair, half)][rows, :]
            if last_of[(pair, j)] == n_units - 1:
                sq = keep[("sq", pair, half)][rows, :]
                nc.scalar.activation(out=sq, in_=acc[(pair, j)][rows, :], func=ACT.Square, scale=rd[rows, 0:1])
                nc.vector.tensor_scalar_mul(out=vec, in0=acc[(pair, j)][rows, :], scalar1=rd[rows, 0:1])
            else:
                nc.scalar.activation(out=vec, in_=acc[(pair, j)][rows, :], func=ACT.Copy, scale=rd[rows, 0:1])

        def square(pair, j):
            if last_of[(pair, j)] == n_units - 1:
                return
            rows = slice(64 * (j // 2), 64 * (j // 2) + 64)
            vec = keep[("vec", pair, j % 2)][rows, :]
            nc.vector.tensor_tensor(out=keep[("sq", pair, j % 2)][rows, :], in0=vec, in1=vec, op=ALU.mult)

        def finish_norm(pair, half):
            bank = psum.tile([P, 512], F32, tag="bank", bufs=6, name="bank")
            nc.tensor.matmul(out=bank[:, 0:P], lhsT=same_image[:], rhs=keep[("sq", pair, half)][:], start=True, stop=True)
            keep[("nsq", pair, half)] = bank

        def finish_root(pair, half):
            rn = tail.tile([P, P], F32, tag="rn", name="rn")
            nc.scalar.activation(out=rn[:], in_=keep[("nsq", pair, half)][:, 0:P], func=ACT.Abs_reciprocal_sqrt)
            keep[("rn", pair, half)] = rn

        def finish_divide(pair, half):
            res = tail.tile([P, P], F32, tag="res", name="res")
            nc.vector.scalar_tensor_tensor(
                out=res[:],
                in0=keep[("rn", pair, half)][:],
                scalar=1.0 / EPS,
                in1=keep[("vec", pair, half)][:],
                op0=ALU.min,
                op1=ALU.mult,
            )
            keep[("res", pair, half)] = res

        def finish_store(pair, half):
            nc.sync.dma_start(
                out=of[P * pair : P * pair + P, P * half : P * half + P], in_=keep[("res", pair, half)][:]
            )

        def live(i):
            return 0 <= i < n_units

        for i in range(-1, n_units + 9):
            for pair in range(2):
                end = last_of[(pair, -1)]
                if i == end + 3:
                    denominator_fold(pair)
                if i == end + 4:
                    denominator_invert(pair)
                for j in TILE_ORDER:
                    end = last_of[(pair, j)]
                    if i == end + 1 + MULTIPLY:
                        read_sums(pair, j)
                    if i == end + 2 + MULTIPLY:
                        square(pair, j)
                    if j >= 2:
                        if i == end + 3 + MULTIPLY:
                            finish_root(pair, j % 2)
                        if i == end + 4 + MULTIPLY:
                            finish_divide(pair, j % 2)
            if live(i + 1):
                shuffle(i + 1)
            if live(i - QUANTISE):
                quantise(i - QUANTISE)
            if live(i):
                transpose_unit(i)
                if i + RAW_BUFS < n_units:
                    start_load(i + RAW_BUFS)
            if live(i - QUANTISE) and units[i - QUANTISE][1] < 0:
                pixel_sums(i - QUANTISE)
            if live(i - MULTIPLY) and units[i - MULTIPLY][1] >= 0:
                mx_unit(i - MULTIPLY)
            for pair in range(2):
                if i == last_of[(pair, -1)] + 3:
                    denominator_place(pair)
                for j in (2, 3):
                    end = last_of[(pair, j)]
                    if i == end + 2 + MULTIPLY:
                        finish_norm(pair, j % 2)
                    if i == end + 4 + MULTIPLY:
                        finish_store(pair, j % 2)
